import numpy as np
import ml_dtypes


def mxq(x, axis, fmt="e4m3"):
    dtype, down = {"e4m3": (ml_dtypes.float8_e4m3fn, 7), "e5m2": (ml_dtypes.float8_e5m2, 14)}[fmt]
    v = np.moveaxis(np.asarray(x, np.float32).astype(ml_dtypes.bfloat16).astype(np.float64), axis, -1)
    blocks = v.reshape(v.shape[:-1] + (-1, 32))
    amax = np.abs(blocks).max(-1, keepdims=True)
    byte = np.maximum(np.where(amax > 0, np.frexp(amax)[1] - 1 + 127, 0) - down, 1)
    scale = np.exp2(byte - 127.0)
    codes = (blocks / scale).astype(np.float32).astype(dtype).astype(np.float64)
    return np.moveaxis((codes * scale).reshape(v.shape), -1, axis)


WIDE = False


def mx_kscale(k):
    if not WIDE:
        return np.ones(k)
    levels = np.array([20, -20, 10, -10, 0])
    a = np.random.permutation(np.resize(levels, k // 512 * 4)).reshape(k // 512, 4)
    idx = np.arange(k)
    return np.exp2(a[idx // 512, idx % 128 // 32])


BF16 = ml_dtypes.bfloat16


def bf(x):
    return np.asarray(x, np.float32).astype(BF16)


def f64(x):
    return np.asarray(x).astype(np.float64)


B, N, AB, MAXN, BB, H = 2, 32, 352, 255, 32, 1024
TAIL = AB - (MAXN + 1)
AF = AB + TAIL
FB = AF + BB + BB
T = B * N * N


def gated_features(f_atoms, f_bonds, adj):
    fa = np.concatenate([f_atoms, f_atoms[:, :, MAXN + 1:]], axis=-1)
    fa_exp = np.broadcast_to(fa[:, :, None, :], (B, N, N, AF))
    fb = np.concatenate([fa_exp, f_bonds, f_bonds], axis=-1)
    return adj[..., None] * fb


def setup_inputs():
    s = mx_kscale(T).reshape(B, N, N)
    f_atoms = np.random.standard_normal((B, N, AB))
    f_bonds = np.random.standard_normal((B, N, N, BB))
    adj = np.random.uniform(size=(B, N, N)) * 4.0 / N * s
    W_i_w = np.random.standard_normal((H, FB)) * 0.1 * N / np.sqrt(FB)
    g = np.random.standard_normal((B, N, N, H)) * np.exp2(np.random.randint(-12, 1, (B, N, N, 1))) / s[..., None]
    return {"f_atoms": bf(f_atoms), "f_bonds": bf(f_bonds), "adj": bf(adj), "W_i_w": bf(W_i_w), "grad_out": bf(g)}


def reference(f_atoms, f_bonds, adj, W_i_w, grad_out):
    gf = gated_features(f64(f_atoms), f64(f_bonds), f64(adj)).reshape(T, FB)
    go = f64(grad_out).reshape(T, H)
    return mxq(go, 0, "e5m2").T @ mxq(gf, 0, "e4m3")

@@ -1,0 +1,183 @@
+import concourse.mybir as mybir
+from concourse.masks import make_identity
+
+BF16 = mybir.dt.bfloat16
+F32 = mybir.dt.float32
+I32 = mybir.dt.int32
+U32 = mybir.dt.uint32
+U8 = mybir.dt.uint8
+E4M3_X4 = mybir.dt.float8_e4m3fn_x4
+E5M2_X4 = mybir.dt.float8_e5m2_x4
+
+P = 128
+PACK = 4
+K_PASS = P * PACK
+TOKENS = 2048
+PASSES = TOKENS // K_PASS
+NEIGHBOURS = 32
+LANES = NEIGHBOURS // PACK
+ATOMS = TOKENS // NEIGHBOURS
+ATOMS_PER_PASS = K_PASS // NEIGHBOURS
+
+H = 1024
+H_TILE = P
+H_UNIT = 512
+UNITS_PER_PASS = H // H_UNIT
+UNITS = UNITS_PER_PASS * PASSES
+TILES_PER_UNIT = H_UNIT // H_TILE
+
+ATOM_F = 352
+TWICE_FROM = 256
+BOND_F = 32
+DISTINCT_F = ATOM_F + BOND_F
+OUT_F = 512
+
+RUN = 4
+SCALAR_COLS = 320
+
+FLOPS = 2 * TOKENS * H * OUT_F
+BYTES = 2 * (ATOMS * ATOM_F + TOKENS * BOND_F + TOKENS + TOKENS * H) + 4 * H * OUT_F
+
+
+def regroup(copy, grouped, raw):
+    copy(
+        out=grouped.rearrange("p (c i) j -> p c j i", i=RUN),
+        in_=raw.rearrange("p j (c i) -> p c j i", i=RUN),
+    )
+
+
+def tile_mpnencoder_pa_kernel(tc, f_atoms, f_bonds, adj, W_i_w, grad_out, out):
+    nc = tc.nc
+    atom_rows = f_atoms.rearrange("b m f -> (b m) f")
+    bond_rows = f_bonds.rearrange("b m n w -> (b m n) w")
+    gates = adj.rearrange("b m n -> (b m n)")
+    grads = grad_out.rearrange("b m n h -> (b m n) h")
+
+    with tc.tile_pool(name="keep", bufs=1) as keep, tc.psum_pool(name="psum", bufs=4) as psum:
+        adj_sb = keep.tile([P, PASSES, PACK], BF16)
+        nc.sync.dma_start(out=adj_sb[:], in_=gates.rearrange("(c p j) -> p c j", p=P, j=PACK))
+        atoms_sb = keep.tile([P, ATOM_F], BF16)
+        nc.sync.dma_start(out=atoms_sb[0:ATOMS, :], in_=atom_rows)
+        bonds_sb = keep.tile([P, PASSES, PACK, BOND_F], BF16)
+        nc.sync.dma_start(
+            out=bonds_sb[:], in_=bond_rows.rearrange("(c p j) w -> p c j w", p=P, j=PACK)
+        )
+        raws = []
+        for u in range(UNITS):
+            half, c = divmod(u, PASSES)
+            raw = keep.tile([P, PACK, H_UNIT], BF16, name="raw%d" % u)
+            nc.sync.dma_start(
+                out=raw[:],
+                in_=grads[
+                    c * K_PASS : (c + 1) * K_PASS, half * H_UNIT : (half + 1) * H_UNIT
+                ].rearrange("(p j) h -> p j h", j=PACK),
+            )
+            raws.append(raw)
+
+        ident = keep.tile([P, P], BF16)
+        make_identity(nc, ident[:])
+        spread = keep.tile([P, ATOMS, LANES], BF16)
+        nc.scalar.copy(
+            out=spread[:], in_=ident[:, 0:ATOMS].unsqueeze(2).to_broadcast([P, ATOMS, LANES])
+        )
+        nc.vector.memset(atoms_sb[ATOMS:P, :].bitcast(I32), 0)
+        atom_pairs = keep.tile([P, ATOM_F, 2], BF16)
+        nc.vector.tensor_copy(
+            out=atom_pairs[:], in_=atoms_sb[:].unsqueeze(2).to_broadcast([P, ATOM_F, 2])
+        )
+
+        g = keep.tile([P, PASSES, DISTINCT_F, PACK], BF16, align_bytes=64)
+        g_codes = keep.tile([P, PASSES, OUT_F], U32, align_bytes=64)
+        g_scales = keep.tile([P, PASSES, OUT_F], U8, align_bytes=64)
+        nc.vector.memset(g_codes[:, :, DISTINCT_F:OUT_F].bitcast(I32), 0)
+        nc.vector.memset(g_scales[:, :, DISTINCT_F:OUT_F].bitcast(I32), 0)
+
+        nc.vector.tensor_tensor(
+            out=g[:, :, ATOM_F:DISTINCT_F, :],
+            in0=bonds_sb[:].rearrange("p c j w -> p c w j"),
+            in1=adj_sb[:].unsqueeze(2).to_broadcast([P, PASSES, BOND_F, PACK]),
+            op=mybir.AluOpType.mult,
+        )
+        half_f = ATOM_F // 2
+        for c in range(PASSES):
+            atoms_here = psum.tile([P, ATOM_F, 2], BF16, tag="atoms_here", name="atoms_here%d" % c)
+            for f0 in (0, half_f):
+                nc.tensor.matmul(
+                    out=atoms_here[:, f0 : f0 + half_f, :].rearrange("p f e -> p (f e)"),
+                    lhsT=spread[:, c * ATOMS_PER_PASS : (c + 1) * ATOMS_PER_PASS, :].rearrange(
+                        "k a i -> k (a i)"
+                    ),
+                    rhs=atom_pairs[:, f0 : f0 + half_f, :].rearrange("k f e -> k (f e)"),
+                    start=True,
+                    stop=True,
+                )
+            nc.vector.tensor_tensor(
+                out=g[:, c, 0:ATOM_F, :].rearrange("p f (a e) -> p f a e", e=2),
+                in0=atoms_here[:].unsqueeze(2).to_broadcast([P, ATOM_F, 2, 2]),
+                in1=adj_sb[:, c, :]
+                .rearrange("p (a e) -> p a e", e=2)
+                .unsqueeze(1)
+                .to_broadcast([P, ATOM_F, 2, 2]),
+                op=mybir.AluOpType.mult,
+            )
+        for c in range(PASSES):
+            for f0, f1 in ((0, 256), (256, DISTINCT_F)):
+                nc.vector.quantize_mx(
+                    out=g_codes[:, c, f0:f1].bitcast(E4M3_X4),
+                    scales=g_scales[:, c, f0:f1],
+                    in_=g[:, c, f0:f1, :].rearrange("p f j -> p (f j)"),
+                )
+
+        go_codes = keep.tile([P, UNITS, H_UNIT], U32, align_bytes=64)
+        go_scales = keep.tile([P, UNITS, H_UNIT], U8, align_bytes=64)
+        groupeds = []
+
+        def regroup_unit(u):
+            grouped = keep.tile([P, H_UNIT, PACK], BF16, name="grouped%d" % u, align_bytes=64)
+            regroup(nc.scalar.copy, grouped[:, 0:SCALAR_COLS, :], raws[u][:, :, 0:SCALAR_COLS])
+            regroup(
+                nc.vector.tensor_copy,
+                grouped[:, SCALAR_COLS:H_UNIT, :],
+                raws[u][:, :, SCALAR_COLS:H_UNIT],
+            )
+            groupeds.append(grouped)
+
+        regroup_unit(0)
+        accs = []
+        for u in range(UNITS):
+            half, c = divmod(u, PASSES)
+            if u + 1 < UNITS:
+                regroup_unit(u + 1)
+            nc.vector.quantize_mx(
+                out=go_codes[:, u, :].bitcast(E5M2_X4),
+                scales=go_scales[:, u, :],
+                in_=groupeds[u][:].rearrange("p h j -> p (h j)"),
+            )
+            for m in range(TILES_PER_UNIT):
+                if c == 0:
+                    acc = psum.tile([P, OUT_F], F32, tag="acc", name="acc%d_%d" % (half, m))
+                    accs.append(acc)
+                acc = accs[half * TILES_PER_UNIT + m]
+                h_cols = slice(m * H_TILE, (m + 1) * H_TILE)
+                nc.tensor.matmul_mx(
+                    out=acc[:],
+                    lhsT=go_codes[:, u, h_cols].bitcast(E5M2_X4),
+                    lhsT_scale=go_scales[:, u, h_cols],
+                    rhs=g_codes[:, c, :].bitcast(E4M3_X4),
+                    rhs_scale=g_scales[:, c, :],
+                    start=(c == 0),
+                    stop=(c == PASSES - 1),
+                )
+                if c == PASSES - 1:
+                    result = keep.tile([P, DISTINCT_F], F32, name="result%d_%d" % (half, m))
+                    if half == UNITS_PER_PASS - 1 and m % 2 == 1:
+                        nc.vector.tensor_copy(out=result[:], in_=acc[:, 0:DISTINCT_F])
+                    else:
+                        nc.scalar.copy(out=result[:], in_=acc[:, 0:DISTINCT_F])
+                    rows = slice(
+                        (half * TILES_PER_UNIT + m) * H_TILE, (half * TILES_PER_UNIT + m + 1) * H_TILE
+                    )
+                    again = ATOM_F + ATOM_F - TWICE_FROM + BOND_F
+                    nc.sync.dma_start(out=out[rows, 0:ATOM_F], in_=result[:, 0:ATOM_F])
+                    nc.sync.dma_start(out=out[rows, ATOM_F:again], in_=result[:, TWICE_FROM:DISTINCT_F])
+                    nc.sync.dma_start(out=out[rows, again:OUT_F], in_=result[:, ATOM_F:DISTINCT_F])

@@ -33,7 +33,8 @@ DISTINCT_F = ATOM_F + BOND_F
 OUT_F = 512
 
 RUN = 4
-SCALAR_COLS = 320
+SCALAR_COLS = 384
+EMPTY_LAG = 3
 
 FLOPS = 2 * TOKENS * H * OUT_F
 BYTES = 2 * (ATOMS * ATOM_F + TOKENS * BOND_F + TOKENS + TOKENS * H) + 4 * H * OUT_F
@@ -53,11 +54,14 @@ def tile_mpnencoder_pa_kernel(tc, f_atoms, f_bonds, adj, W_i_w, grad_out, out):
     gates = adj.rearrange("b m n -> (b m n)")
     grads = grad_out.rearrange("b m n h -> (b m n) h")
 
-    with tc.tile_pool(name="keep", bufs=1) as keep, tc.psum_pool(name="psum", bufs=4) as psum:
-        adj_sb = keep.tile([P, PASSES, PACK], BF16)
-        nc.sync.dma_start(out=adj_sb[:], in_=gates.rearrange("(c p j) -> p c j", p=P, j=PACK))
+    with tc.tile_pool(name="keep", bufs=1) as keep, tc.psum_pool(
+        name="psum", bufs=1
+    ) as psum, tc.manual_schedule():
+
         atoms_sb = keep.tile([P, ATOM_F], BF16)
         nc.sync.dma_start(out=atoms_sb[0:ATOMS, :], in_=atom_rows)
+        adj_sb = keep.tile([P, PASSES, PACK], BF16)
+        nc.sync.dma_start(out=adj_sb[:], in_=gates.rearrange("(c p j) -> p c j", p=P, j=PACK))
         bonds_sb = keep.tile([P, PASSES, PACK, BOND_F], BF16)
         nc.sync.dma_start(
             out=bonds_sb[:], in_=bond_rows.rearrange("(c p j) w -> p c j w", p=P, j=PACK)
@@ -81,26 +85,33 @@ def tile_mpnencoder_pa_kernel(tc, f_atoms, f_bonds, adj, W_i_w, grad_out, out):
             out=spread[:], in_=ident[:, 0:ATOMS].unsqueeze(2).to_broadcast([P, ATOMS, LANES])
         )
         nc.vector.memset(atoms_sb[ATOMS:P, :].bitcast(I32), 0)
-        atom_pairs = keep.tile([P, ATOM_F, 2], BF16)
-        nc.vector.tensor_copy(
-            out=atom_pairs[:], in_=atoms_sb[:].unsqueeze(2).to_broadcast([P, ATOM_F, 2])
-        )
-
         g = keep.tile([P, PASSES, DISTINCT_F, PACK], BF16, align_bytes=64)
         g_codes = keep.tile([P, PASSES, OUT_F], U32, align_bytes=64)
         g_scales = keep.tile([P, PASSES, OUT_F], U8, align_bytes=64)
         nc.vector.memset(g_codes[:, :, DISTINCT_F:OUT_F].bitcast(I32), 0)
         nc.vector.memset(g_scales[:, :, DISTINCT_F:OUT_F].bitcast(I32), 0)
-
+        atom_pairs = keep.tile([P, ATOM_F, 2], BF16)
+        nc.scalar.copy(
+            out=atom_pairs[:], in_=atoms_sb[:].unsqueeze(2).to_broadcast([P, ATOM_F, 2])
+        )
         nc.vector.tensor_tensor(
             out=g[:, :, ATOM_F:DISTINCT_F, :],
             in0=bonds_sb[:].rearrange("p c j w -> p c w j"),
             in1=adj_sb[:].unsqueeze(2).to_broadcast([P, PASSES, BOND_F, PACK]),
             op=mybir.AluOpType.mult,
         )
-        half_f = ATOM_F // 2
+
+        go_codes = keep.tile([P, UNITS, H_UNIT], U32, align_bytes=64)
+        go_scales = keep.tile([P, UNITS, H_UNIT], U8, align_bytes=64)
+        groupeds = []
+        accs = []
+
+        atoms_heres = []
         for c in range(PASSES):
-            atoms_here = psum.tile([P, ATOM_F, 2], BF16, tag="atoms_here", name="atoms_here%d" % c)
+            atoms_here = psum.tile(
+                [P, ATOM_F, 2], BF16, tag="bank%d" % (TILES_PER_UNIT + c), name="atoms_here%d" % c
+            )
+            half_f = ATOM_F // 2
             for f0 in (0, half_f):
                 nc.tensor.matmul(
                     out=atoms_here[:, f0 : f0 + half_f, :].rearrange("p f e -> p (f e)"),
@@ -111,26 +122,26 @@ def tile_mpnencoder_pa_kernel(tc, f_atoms, f_bonds, adj, W_i_w, grad_out, out):
                     start=True,
                     stop=True,
                 )
+            atoms_heres.append(atoms_here)
+
+        def gate_atoms(c):
             nc.vector.tensor_tensor(
                 out=g[:, c, 0:ATOM_F, :].rearrange("p f (a e) -> p f a e", e=2),
-                in0=atoms_here[:].unsqueeze(2).to_broadcast([P, ATOM_F, 2, 2]),
+                in0=atoms_heres[c][:].unsqueeze(2).to_broadcast([P, ATOM_F, 2, 2]),
                 in1=adj_sb[:, c, :]
                 .rearrange("p (a e) -> p a e", e=2)
                 .unsqueeze(1)
                 .to_broadcast([P, ATOM_F, 2, 2]),
                 op=mybir.AluOpType.mult,
             )
-        for c in range(PASSES):
+
+        def quantise_features(c):
             for f0, f1 in ((0, 256), (256, DISTINCT_F)):
                 nc.vector.quantize_mx(
                     out=g_codes[:, c, f0:f1].bitcast(E4M3_X4),
                     scales=g_scales[:, c, f0:f1],
                     in_=g[:, c, f0:f1, :].rearrange("p f j -> p (f j)"),
                 )
-
-        go_codes = keep.tile([P, UNITS, H_UNIT], U32, align_bytes=64)
-        go_scales = keep.tile([P, UNITS, H_UNIT], U8, align_bytes=64)
-        groupeds = []
 
         def regroup_unit(u):
             grouped = keep.tile([P, H_UNIT, PACK], BF16, name="grouped%d" % u, align_bytes=64)
@@ -142,25 +153,23 @@ def tile_mpnencoder_pa_kernel(tc, f_atoms, f_bonds, adj, W_i_w, grad_out, out):
             )
             groupeds.append(grouped)
 
-        regroup_unit(0)
-        accs = []
-        for u in range(UNITS):
-            half, c = divmod(u, PASSES)
-            if u + 1 < UNITS:
-                regroup_unit(u + 1)
+        def quantise_gradient(u):
             nc.vector.quantize_mx(
                 out=go_codes[:, u, :].bitcast(E5M2_X4),
                 scales=go_scales[:, u, :],
                 in_=groupeds[u][:].rearrange("p h j -> p (h j)"),
             )
+
+        def multiply(u):
+            half, c = divmod(u, PASSES)
             for m in range(TILES_PER_UNIT):
+                t = half * TILES_PER_UNIT + m
                 if c == 0:
-                    acc = psum.tile([P, OUT_F], F32, tag="acc", name="acc%d_%d" % (half, m))
+                    acc = psum.tile([P, OUT_F], F32, tag="bank%d" % t, name="acc%d" % t)
                     accs.append(acc)
-                acc = accs[half * TILES_PER_UNIT + m]
                 h_cols = slice(m * H_TILE, (m + 1) * H_TILE)
                 nc.tensor.matmul_mx(
-                    out=acc[:],
+                    out=accs[t][:],
                     lhsT=go_codes[:, u, h_cols].bitcast(E5M2_X4),
                     lhsT_scale=go_scales[:, u, h_cols],
                     rhs=g_codes[:, c, :].bitcast(E4M3_X4),
@@ -168,16 +177,33 @@ def tile_mpnencoder_pa_kernel(tc, f_atoms, f_bonds, adj, W_i_w, grad_out, out):
                     start=(c == 0),
                     stop=(c == PASSES - 1),
                 )
-                if c == PASSES - 1:
-                    result = keep.tile([P, DISTINCT_F], F32, name="result%d_%d" % (half, m))
-                    if half == UNITS_PER_PASS - 1 and m % 2 == 1:
-                        nc.vector.tensor_copy(out=result[:], in_=acc[:, 0:DISTINCT_F])
-                    else:
-                        nc.scalar.copy(out=result[:], in_=acc[:, 0:DISTINCT_F])
-                    rows = slice(
-                        (half * TILES_PER_UNIT + m) * H_TILE, (half * TILES_PER_UNIT + m + 1) * H_TILE
-                    )
-                    again = ATOM_F + ATOM_F - TWICE_FROM + BOND_F
-                    nc.sync.dma_start(out=out[rows, 0:ATOM_F], in_=result[:, 0:ATOM_F])
-                    nc.sync.dma_start(out=out[rows, ATOM_F:again], in_=result[:, TWICE_FROM:DISTINCT_F])
-                    nc.sync.dma_start(out=out[rows, again:OUT_F], in_=result[:, ATOM_F:DISTINCT_F])
+
+        def empty_banks(half):
+            for m in range(TILES_PER_UNIT):
+                t = half * TILES_PER_UNIT + m
+                result = keep.tile([P, DISTINCT_F], F32, name="result%d" % t)
+                if t % 2 == 0:
+                    nc.scalar.copy(out=result[:], in_=accs[t][:, 0:DISTINCT_F])
+                else:
+                    nc.vector.tensor_copy(out=result[:], in_=accs[t][:, 0:DISTINCT_F])
+                rows = slice(t * H_TILE, (t + 1) * H_TILE)
+                again = ATOM_F + ATOM_F - TWICE_FROM + BOND_F
+                nc.sync.dma_start(out=out[rows, 0:ATOM_F], in_=result[:, 0:ATOM_F])
+                nc.sync.dma_start(out=out[rows, ATOM_F:again], in_=result[:, TWICE_FROM:DISTINCT_F])
+                nc.sync.dma_start(out=out[rows, again:OUT_F], in_=result[:, ATOM_F:DISTINCT_F])
+
+        regroup_unit(0)
+        gate_atoms(0)
+        for step in range(UNITS + EMPTY_LAG):
+            if step + 1 < PASSES:
+                gate_atoms(step + 1)
+            if step < PASSES:
+                quantise_features(step)
+            if step + 1 < UNITS:
+                regroup_unit(step + 1)
+            if step < UNITS:
+                quantise_gradient(step)
+                multiply(step)
+            done = step - EMPTY_LAG
+            if done >= 0 and done % PASSES == PASSES - 1:
+                empty_banks(done // PASSES)

@@ -21,10 +21,7 @@ ATOMS_PER_PASS = K_PASS // NEIGHBOURS
 
 H = 1024
 H_TILE = P
-H_UNIT = 512
-UNITS_PER_PASS = H // H_UNIT
-UNITS = UNITS_PER_PASS * PASSES
-TILES_PER_UNIT = H_UNIT // H_TILE
+H_GROUPS = (512, 256, 256)
 
 ATOM_F = 352
 TWICE_FROM = 256
@@ -33,8 +30,8 @@ DISTINCT_F = ATOM_F + BOND_F
 OUT_F = 512
 
 RUN = 4
-SCALAR_COLS = 384
-EMPTY_LAG = 3
+SCALAR_SIXTEENTHS = 12
+EMPTY_LAG = 2
 
 FLOPS = 2 * TOKENS * H * OUT_F
 BYTES = 2 * (ATOMS * ATOM_F + TOKENS * BOND_F + TOKENS + TOKENS * H) + 4 * H * OUT_F
@@ -66,15 +63,18 @@ def tile_mpnencoder_pa_kernel(tc, f_atoms, f_bonds, adj, W_i_w, grad_out, out):
         nc.sync.dma_start(
             out=bonds_sb[:], in_=bond_rows.rearrange("(c p j) w -> p c j w", p=P, j=PACK)
         )
+        units = []
+        for i, width in enumerate(H_GROUPS):
+            for c in range(PASSES):
+                units.append((sum(H_GROUPS[0:i]), width, c))
         raws = []
-        for u in range(UNITS):
-            half, c = divmod(u, PASSES)
-            raw = keep.tile([P, PACK, H_UNIT], BF16, name="raw%d" % u)
+        for u, (h0, width, c) in enumerate(units):
+            raw = keep.tile([P, PACK, width], BF16, name="raw%d" % u)
             nc.sync.dma_start(
                 out=raw[:],
-                in_=grads[
-                    c * K_PASS : (c + 1) * K_PASS, half * H_UNIT : (half + 1) * H_UNIT
-                ].rearrange("(p j) h -> p j h", j=PACK),
+                in_=grads[c * K_PASS : (c + 1) * K_PASS, h0 : h0 + width].rearrange(
+                    "(p j) h -> p j h", j=PACK
+                ),
             )
             raws.append(raw)
 
@@ -101,15 +101,15 @@ def tile_mpnencoder_pa_kernel(tc, f_atoms, f_bonds, adj, W_i_w, grad_out, out):
             op=mybir.AluOpType.mult,
         )
 
-        go_codes = keep.tile([P, UNITS, H_UNIT], U32, align_bytes=64)
-        go_scales = keep.tile([P, UNITS, H_UNIT], U8, align_bytes=64)
+        go_codes = keep.tile([P, PASSES, H], U32, align_bytes=64)
+        go_scales = keep.tile([P, PASSES, H], U8, align_bytes=64)
         groupeds = []
         accs = []
 
         atoms_heres = []
         for c in range(PASSES):
             atoms_here = psum.tile(
-                [P, ATOM_F, 2], BF16, tag="bank%d" % (TILES_PER_UNIT + c), name="atoms_here%d" % c
+                [P, ATOM_F, 2], BF16, tag="bank%d" % (PASSES + c), name="atoms_here%d" % c
             )
             half_f = ATOM_F // 2
             for f0 in (0, half_f):
@@ -144,45 +144,47 @@ def tile_mpnencoder_pa_kernel(tc, f_atoms, f_bonds, adj, W_i_w, grad_out, out):
                 )
 
         def regroup_unit(u):
-            grouped = keep.tile([P, H_UNIT, PACK], BF16, name="grouped%d" % u, align_bytes=64)
-            regroup(nc.scalar.copy, grouped[:, 0:SCALAR_COLS, :], raws[u][:, :, 0:SCALAR_COLS])
+            h0, width, c = units[u]
+            scalar_cols = width * SCALAR_SIXTEENTHS // 16
+            grouped = keep.tile([P, width, PACK], BF16, name="grouped%d" % u, align_bytes=64)
+            regroup(nc.scalar.copy, grouped[:, 0:scalar_cols, :], raws[u][:, :, 0:scalar_cols])
             regroup(
                 nc.vector.tensor_copy,
-                grouped[:, SCALAR_COLS:H_UNIT, :],
-                raws[u][:, :, SCALAR_COLS:H_UNIT],
+                grouped[:, scalar_cols:width, :],
+                raws[u][:, :, scalar_cols:width],
             )
             groupeds.append(grouped)
 
         def quantise_gradient(u):
+            h0, width, c = units[u]
             nc.vector.quantize_mx(
-                out=go_codes[:, u, :].bitcast(E5M2_X4),
-                scales=go_scales[:, u, :],
+                out=go_codes[:, c, h0 : h0 + width].bitcast(E5M2_X4),
+                scales=go_scales[:, c, h0 : h0 + width],
                 in_=groupeds[u][:].rearrange("p h j -> p (h j)"),
             )
 
         def multiply(u):
-            half, c = divmod(u, PASSES)
-            for m in range(TILES_PER_UNIT):
-                t = half * TILES_PER_UNIT + m
+            h0, width, c = units[u]
+            for t in range(h0 // H_TILE, (h0 + width) // H_TILE):
                 if c == 0:
                     acc = psum.tile([P, OUT_F], F32, tag="bank%d" % t, name="acc%d" % t)
                     accs.append(acc)
-                h_cols = slice(m * H_TILE, (m + 1) * H_TILE)
+                h_cols = slice(t * H_TILE, (t + 1) * H_TILE)
                 nc.tensor.matmul_mx(
                     out=accs[t][:],
-                    lhsT=go_codes[:, u, h_cols].bitcast(E5M2_X4),
-                    lhsT_scale=go_scales[:, u, h_cols],
+                    lhsT=go_codes[:, c, h_cols].bitcast(E5M2_X4),
+                    lhsT_scale=go_scales[:, c, h_cols],
                     rhs=g_codes[:, c, :].bitcast(E4M3_X4),
                     rhs_scale=g_scales[:, c, :],
                     start=(c == 0),
                     stop=(c == PASSES - 1),
                 )
 
-        def empty_banks(half):
-            for m in range(TILES_PER_UNIT):
-                t = half * TILES_PER_UNIT + m
+        def empty_banks(u):
+            h0, width, c = units[u]
+            for t in range(h0 // H_TILE, (h0 + width) // H_TILE):
                 result = keep.tile([P, DISTINCT_F], F32, name="result%d" % t)
-                if t % 2 == 0:
+                if u == len(units) - 1 and t % 2 == 0:
                     nc.scalar.copy(out=result[:], in_=accs[t][:, 0:DISTINCT_F])
                 else:
                     nc.vector.tensor_copy(out=result[:], in_=accs[t][:, 0:DISTINCT_F])
@@ -194,16 +196,16 @@ def tile_mpnencoder_pa_kernel(tc, f_atoms, f_bonds, adj, W_i_w, grad_out, out):
 
         regroup_unit(0)
         gate_atoms(0)
-        for step in range(UNITS + EMPTY_LAG):
+        for step in range(len(units) + EMPTY_LAG):
             if step + 1 < PASSES:
                 gate_atoms(step + 1)
             if step < PASSES:
                 quantise_features(step)
-            if step + 1 < UNITS:
+            if step + 1 < len(units):
                 regroup_unit(step + 1)
-            if step < UNITS:
+            if step < len(units):
                 quantise_gradient(step)
                 multiply(step)
             done = step - EMPTY_LAG
             if done >= 0 and done % PASSES == PASSES - 1:
-                empty_banks(done // PASSES)
+                empty_banks(done)

@@ -31,7 +31,7 @@ OUT_F = 512
 
 RUN = 4
 SCALAR_SIXTEENTHS = 12
-EMPTY_LAG = 2
+EMPTY_LAG = 3
 
 FLOPS = 2 * TOKENS * H * OUT_F
 BYTES = 2 * (ATOMS * ATOM_F + TOKENS * BOND_F + TOKENS + TOKENS * H) + 4 * H * OUT_F
@@ -184,7 +184,7 @@ def tile_mpnencoder_pa_kernel(tc, f_atoms, f_bonds, adj, W_i_w, grad_out, out):
             h0, width, c = units[u]
             for t in range(h0 // H_TILE, (h0 + width) // H_TILE):
                 result = keep.tile([P, DISTINCT_F], F32, name="result%d" % t)
-                if u == len(units) - 1 and t % 2 == 0:
+                if t % 2 == 0:
                     nc.scalar.copy(out=result[:], in_=accs[t][:, 0:DISTINCT_F])
                 else:
                     nc.vector.tensor_copy(out=result[:], in_=accs[t][:, 0:DISTINCT_F])

@@ -30,7 +30,7 @@ DISTINCT_F = ATOM_F + BOND_F
 OUT_F = 512
 
 RUN = 4
-SCALAR_SIXTEENTHS = 12
+SCALAR_SIXTEENTHS = 11
 EMPTY_LAG = 3
 
 FLOPS = 2 * TOKENS * H * OUT_F

@@ -31,6 +31,9 @@ OUT_F = 512
 
 RUN = 4
 SCALAR_SIXTEENTHS = 11
+FIRST_PIECES = 2
+LAST_PIECES = 2
+WARM_UP = 3
 EMPTY_LAG = 3
 
 FLOPS = 2 * TOKENS * H * OUT_F
@@ -63,20 +66,32 @@ def tile_mpnencoder_pa_kernel(tc, f_atoms, f_bonds, adj, W_i_w, grad_out, out):
         nc.sync.dma_start(
             out=bonds_sb[:], in_=bond_rows.rearrange("(c p j) w -> p c j w", p=P, j=PACK)
         )
-        units = []
+        loads = []
         for i, width in enumerate(H_GROUPS):
             for c in range(PASSES):
-                units.append((sum(H_GROUPS[0:i]), width, c))
+                loads.append((sum(H_GROUPS[0:i]), width, c))
+        units = []
         raws = []
-        for u, (h0, width, c) in enumerate(units):
-            raw = keep.tile([P, PACK, width], BF16, name="raw%d" % u)
-            nc.sync.dma_start(
-                out=raw[:],
-                in_=grads[c * K_PASS : (c + 1) * K_PASS, h0 : h0 + width].rearrange(
-                    "(p j) h -> p j h", j=PACK
-                ),
-            )
-            raws.append(raw)
+        for n, (h0, width, c) in enumerate(loads):
+            tiles = []
+            tile_cols = width // (FIRST_PIECES if n == 0 else 1)
+            for first in range(0, width, tile_cols):
+                raw = keep.tile([P, PACK, tile_cols], BF16, name="raw%d_%d" % (n, first))
+                nc.sync.dma_start(
+                    out=raw[:],
+                    in_=grads[
+                        c * K_PASS : (c + 1) * K_PASS, h0 + first : h0 + first + tile_cols
+                    ].rearrange("(p j) h -> p j h", j=PACK),
+                )
+                tiles.append((first, first + tile_cols, raw, 0))
+            if n == len(loads) - 1:
+                unit_cols = width // LAST_PIECES
+                for first in range(0, width, unit_cols):
+                    units.append((h0 + first, unit_cols, c))
+                    raws.append([(0, unit_cols, tiles[0][2], first)])
+            else:
+                units.append((h0, width, c))
+                raws.append(tiles)
 
         ident = keep.tile([P, P], BF16)
         make_identity(nc, ident[:])
@@ -90,10 +105,6 @@ def tile_mpnencoder_pa_kernel(tc, f_atoms, f_bonds, adj, W_i_w, grad_out, out):
         g_scales = keep.tile([P, PASSES, OUT_F], U8, align_bytes=64)
         nc.vector.memset(g_codes[:, :, DISTINCT_F:OUT_F].bitcast(I32), 0)
         nc.vector.memset(g_scales[:, :, DISTINCT_F:OUT_F].bitcast(I32), 0)
-        atom_pairs = keep.tile([P, ATOM_F, 2], BF16)
-        nc.scalar.copy(
-            out=atom_pairs[:], in_=atoms_sb[:].unsqueeze(2).to_broadcast([P, ATOM_F, 2])
-        )
         nc.vector.tensor_tensor(
             out=g[:, :, ATOM_F:DISTINCT_F, :],
             in0=bonds_sb[:].rearrange("p c j w -> p c w j"),
@@ -106,6 +117,16 @@ def tile_mpnencoder_pa_kernel(tc, f_atoms, f_bonds, adj, W_i_w, grad_out, out):
         groupeds = []
         accs = []
 
+        warm = psum.tile([P, OUT_F // P, P], F32, tag="bank0", name="warm")
+        for i in range(WARM_UP):
+            nc.tensor.matmul(
+                out=warm[:],
+                lhsT=ident[:],
+                rhs=ident[:].unsqueeze(1).to_broadcast([P, OUT_F // P, P]),
+                start=True,
+                stop=True,
+            )
+
         atoms_heres = []
         for c in range(PASSES):
             atoms_here = psum.tile(
@@ -114,11 +135,11 @@ def tile_mpnencoder_pa_kernel(tc, f_atoms, f_bonds, adj, W_i_w, grad_out, out):
             half_f = ATOM_F // 2
             for f0 in (0, half_f):
                 nc.tensor.matmul(
-                    out=atoms_here[:, f0 : f0 + half_f, :].rearrange("p f e -> p (f e)"),
+                    out=atoms_here[:, f0 : f0 + half_f, :],
                     lhsT=spread[:, c * ATOMS_PER_PASS : (c + 1) * ATOMS_PER_PASS, :].rearrange(
                         "k a i -> k (a i)"
                     ),
-                    rhs=atom_pairs[:, f0 : f0 + half_f, :].rearrange("k f e -> k (f e)"),
+                    rhs=atoms_sb[:, f0 : f0 + half_f].unsqueeze(2).to_broadcast([P, half_f, 2]),
                     start=True,
                     stop=True,
                 )
@@ -147,12 +168,18 @@ def tile_mpnencoder_pa_kernel(tc, f_atoms, f_bonds, adj, W_i_w, grad_out, out):
             h0, width, c = units[u]
             scalar_cols = width * SCALAR_SIXTEENTHS // 16
             grouped = keep.tile([P, width, PACK], BF16, name="grouped%d" % u, align_bytes=64)
-            regroup(nc.scalar.copy, grouped[:, 0:scalar_cols, :], raws[u][:, :, 0:scalar_cols])
-            regroup(
-                nc.vector.tensor_copy,
-                grouped[:, scalar_cols:width, :],
-                raws[u][:, :, scalar_cols:width],
-            )
+            for first, end, raw, r0 in raws[u]:
+                cut = min(max(scalar_cols, first), end)
+                if cut > first:
+                    regroup(
+                        nc.scalar.copy, grouped[:, first:cut, :], raw[:, :, r0 : r0 + cut - first]
+                    )
+                if end > cut:
+                    regroup(
+                        nc.vector.tensor_copy,
+                        grouped[:, cut:end, :],
+                        raw[:, :, r0 + cut - first : r0 + end - first],
+                    )
             groupeds.append(grouped)
 
         def quantise_gradient(u):
@@ -194,8 +221,8 @@ def tile_mpnencoder_pa_kernel(tc, f_atoms, f_bonds, adj, W_i_w, grad_out, out):
                 nc.sync.dma_start(out=out[rows, ATOM_F:again], in_=result[:, TWICE_FROM:DISTINCT_F])
                 nc.sync.dma_start(out=out[rows, again:OUT_F], in_=result[:, ATOM_F:DISTINCT_F])
 
-        regroup_unit(0)
         gate_atoms(0)
+        regroup_unit(0)
         for step in range(len(units) + EMPTY_LAG):
             if step + 1 < PASSES:
                 gate_atoms(step + 1)
@@ -207,5 +234,5 @@ def tile_mpnencoder_pa_kernel(tc, f_atoms, f_bonds, adj, W_i_w, grad_out, out):
                 quantise_gradient(step)
                 multiply(step)
             done = step - EMPTY_LAG
-            if done >= 0 and done % PASSES == PASSES - 1:
+            if done >= 0 and units[done][2] == PASSES - 1:
                 empty_banks(done)

@@ -30,7 +30,7 @@ DISTINCT_F = ATOM_F + BOND_F
 OUT_F = 512
 
 RUN = 4
-SCALAR_SIXTEENTHS = 11
+SCALAR_SIXTEENTHS = (13, 7, 7)
 FIRST_PIECES = 2
 LAST_PIECES = 2
 WARM_UP = 3
@@ -166,7 +166,7 @@ def tile_mpnencoder_pa_kernel(tc, f_atoms, f_bonds, adj, W_i_w, grad_out, out):
 
         def regroup_unit(u):
             h0, width, c = units[u]
-            scalar_cols = width * SCALAR_SIXTEENTHS // 16
+            scalar_cols = width * SCALAR_SIXTEENTHS[min(u // PASSES, len(H_GROUPS) - 1)] // 16
             grouped = keep.tile([P, width, PACK], BF16, name="grouped%d" % u, align_bytes=64)
             for first, end, raw, r0 in raws[u]:
                 cut = min(max(scalar_cols, first), end)
@@ -211,7 +211,7 @@ def tile_mpnencoder_pa_kernel(tc, f_atoms, f_bonds, adj, W_i_w, grad_out, out):
             h0, width, c = units[u]
             for t in range(h0 // H_TILE, (h0 + width) // H_TILE):
                 result = keep.tile([P, DISTINCT_F], F32, name="result%d" % t)
-                if t % 2 == 0:
+                if t < H // H_TILE - 1:
                     nc.scalar.copy(out=result[:], in_=accs[t][:, 0:DISTINCT_F])
                 else:
                     nc.vector.tensor_copy(out=result[:], in_=accs[t][:, 0:DISTINCT_F])

@@ -29,7 +29,7 @@ BOND_F = 32
 DISTINCT_F = ATOM_F + BOND_F
 OUT_F = 512
 
-RUN = 4
+RUN = 8
 SCALAR_SIXTEENTHS = (13, 7, 7)
 FIRST_PIECES = 2
 LAST_PIECES = 2

@@ -105,7 +105,7 @@ def tile_mpnencoder_pa_kernel(tc, f_atoms, f_bonds, adj, W_i_w, grad_out, out):
         g_scales = keep.tile([P, PASSES, OUT_F], U8, align_bytes=64)
         nc.vector.memset(g_codes[:, :, DISTINCT_F:OUT_F].bitcast(I32), 0)
         nc.vector.memset(g_scales[:, :, DISTINCT_F:OUT_F].bitcast(I32), 0)
-        nc.vector.tensor_tensor(
+        nc.gpsimd.tensor_tensor(
             out=g[:, :, ATOM_F:DISTINCT_F, :],
             in0=bonds_sb[:].rearrange("p c j w -> p c w j"),
             in1=adj_sb[:].unsqueeze(2).to_broadcast([P, PASSES, BOND_F, PACK]),

@@ -30,7 +30,7 @@ DISTINCT_F = ATOM_F + BOND_F
 OUT_F = 512
 
 RUN = 8
-SCALAR_SIXTEENTHS = (13, 7, 7)
+SCALAR_SIXTEENTHS = (13, 6, 6)
 FIRST_PIECES = 2
 LAST_PIECES = 2
 WARM_UP = 3

@@ -30,7 +30,7 @@ DISTINCT_F = ATOM_F + BOND_F
 OUT_F = 512
 
 RUN = 8
-SCALAR_SIXTEENTHS = (13, 6, 6)
+SCALAR_SIXTEENTHS = (13, 7, 6)
 FIRST_PIECES = 2
 LAST_PIECES = 2
 WARM_UP = 3

import concourse.mybir as mybir
from concourse.masks import make_identity

BF16 = mybir.dt.bfloat16
F32 = mybir.dt.float32
I32 = mybir.dt.int32
U32 = mybir.dt.uint32
U8 = mybir.dt.uint8
E4M3_X4 = mybir.dt.float8_e4m3fn_x4
E5M2_X4 = mybir.dt.float8_e5m2_x4

P = 128
PACK = 4
K_PASS = P * PACK
TOKENS = 2048
PASSES = TOKENS // K_PASS
NEIGHBOURS = 32
LANES = NEIGHBOURS // PACK
ATOMS = TOKENS // NEIGHBOURS
ATOMS_PER_PASS = K_PASS // NEIGHBOURS

H = 1024
H_TILE = P
H_GROUPS = (512, 256, 256)

ATOM_F = 352
TWICE_FROM = 256
BOND_F = 32
DISTINCT_F = ATOM_F + BOND_F
OUT_F = 512

RUN = 8
SCALAR_SIXTEENTHS = (13, 7, 6)
FIRST_PIECES = 2
LAST_PIECES = 2
WARM_UP = 3
EMPTY_LAG = 3

FLOPS = 2 * TOKENS * H * OUT_F
BYTES = 2 * (ATOMS * ATOM_F + TOKENS * BOND_F + TOKENS + TOKENS * H) + 4 * H * OUT_F


def regroup(copy, grouped, raw):
    copy(
        out=grouped.rearrange("p (c i) j -> p c j i", i=RUN),
        in_=raw.rearrange("p j (c i) -> p c j i", i=RUN),
    )


def tile_mpnencoder_pa_kernel(tc, f_atoms, f_bonds, adj, W_i_w, grad_out, out):
    nc = tc.nc
    atom_rows = f_atoms.rearrange("b m f -> (b m) f")
    bond_rows = f_bonds.rearrange("b m n w -> (b m n) w")
    gates = adj.rearrange("b m n -> (b m n)")
    grads = grad_out.rearrange("b m n h -> (b m n) h")

    with tc.tile_pool(name="keep", bufs=1) as keep, tc.psum_pool(
        name="psum", bufs=1
    ) as psum, tc.manual_schedule():

        atoms_sb = keep.tile([P, ATOM_F], BF16)
        nc.sync.dma_start(out=atoms_sb[0:ATOMS, :], in_=atom_rows)
        adj_sb = keep.tile([P, PASSES, PACK], BF16)
        nc.sync.dma_start(out=adj_sb[:], in_=gates.rearrange("(c p j) -> p c j", p=P, j=PACK))
        bonds_sb = keep.tile([P, PASSES, PACK, BOND_F], BF16)
        nc.sync.dma_start(
            out=bonds_sb[:], in_=bond_rows.rearrange("(c p j) w -> p c j w", p=P, j=PACK)
        )
        loads = []
        for i, width in enumerate(H_GROUPS):
            for c in range(PASSES):
                loads.append((sum(H_GROUPS[0:i]), width, c))
        units = []
        raws = []
        for n, (h0, width, c) in enumerate(loads):
            tiles = []
            tile_cols = width // (FIRST_PIECES if n == 0 else 1)
            for first in range(0, width, tile_cols):
                raw = keep.tile([P, PACK, tile_cols], BF16, name="raw%d_%d" % (n, first))
                nc.sync.dma_start(
                    out=raw[:],
                    in_=grads[
                        c * K_PASS : (c + 1) * K_PASS, h0 + first : h0 + first + tile_cols
                    ].rearrange("(p j) h -> p j h", j=PACK),
                )
                tiles.append((first, first + tile_cols, raw, 0))
            if n == len(loads) - 1:
                unit_cols = width // LAST_PIECES
                for first in range(0, width, unit_cols):
                    units.append((h0 + first, unit_cols, c))
                    raws.append([(0, unit_cols, tiles[0][2], first)])
            else:
                units.append((h0, width, c))
                raws.append(tiles)

        ident = keep.tile([P, P], BF16)
        make_identity(nc, ident[:])
        spread = keep.tile([P, ATOMS, LANES], BF16)
        nc.scalar.copy(
            out=spread[:], in_=ident[:, 0:ATOMS].unsqueeze(2).to_broadcast([P, ATOMS, LANES])
        )
        nc.vector.memset(atoms_sb[ATOMS:P, :].bitcast(I32), 0)
        g = keep.tile([P, PASSES, DISTINCT_F, PACK], BF16, align_bytes=64)
        g_codes = keep.tile([P, PASSES, OUT_F], U32, align_bytes=64)
        g_scales = keep.tile([P, PASSES, OUT_F], U8, align_bytes=64)
        nc.vector.memset(g_codes[:, :, DISTINCT_F:OUT_F].bitcast(I32), 0)
        nc.vector.memset(g_scales[:, :, DISTINCT_F:OUT_F].bitcast(I32), 0)
        nc.gpsimd.tensor_tensor(
            out=g[:, :, ATOM_F:DISTINCT_F, :],
            in0=bonds_sb[:].rearrange("p c j w -> p c w j"),
            in1=adj_sb[:].unsqueeze(2).to_broadcast([P, PASSES, BOND_F, PACK]),
            op=mybir.AluOpType.mult,
        )

        go_codes = keep.tile([P, PASSES, H], U32, align_bytes=64)
        go_scales = keep.tile([P, PASSES, H], U8, align_bytes=64)
        groupeds = []
        accs = []

        warm = psum.tile([P, OUT_F // P, P], F32, tag="bank0", name="warm")
        for i in range(WARM_UP):
            nc.tensor.matmul(
                out=warm[:],
                lhsT=ident[:],
                rhs=ident[:].unsqueeze(1).to_broadcast([P, OUT_F // P, P]),
                start=True,
                stop=True,
            )

        atoms_heres = []
        for c in range(PASSES):
            atoms_here = psum.tile(
                [P, ATOM_F, 2], BF16, tag="bank%d" % (PASSES + c), name="atoms_here%d" % c
            )
            half_f = ATOM_F // 2
            for f0 in (0, half_f):
                nc.tensor.matmul(
                    out=atoms_here[:, f0 : f0 + half_f, :],
                    lhsT=spread[:, c * ATOMS_PER_PASS : (c + 1) * ATOMS_PER_PASS, :].rearrange(
                        "k a i -> k (a i)"
                    ),
                    rhs=atoms_sb[:, f0 : f0 + half_f].unsqueeze(2).to_broadcast([P, half_f, 2]),
                    start=True,
                    stop=True,
                )
            atoms_heres.append(atoms_here)

        def gate_atoms(c):
            nc.vector.tensor_tensor(
                out=g[:, c, 0:ATOM_F, :].rearrange("p f (a e) -> p f a e", e=2),
                in0=atoms_heres[c][:].unsqueeze(2).to_broadcast([P, ATOM_F, 2, 2]),
                in1=adj_sb[:, c, :]
                .rearrange("p (a e) -> p a e", e=2)
                .unsqueeze(1)
                .to_broadcast([P, ATOM_F, 2, 2]),
                op=mybir.AluOpType.mult,
            )

        def quantise_features(c):
            for f0, f1 in ((0, 256), (256, DISTINCT_F)):
                nc.vector.quantize_mx(
                    out=g_codes[:, c, f0:f1].bitcast(E4M3_X4),
                    scales=g_scales[:, c, f0:f1],
                    in_=g[:, c, f0:f1, :].rearrange("p f j -> p (f j)"),
                )

        def regroup_unit(u):
            h0, width, c = units[u]
            scalar_cols = width * SCALAR_SIXTEENTHS[min(u // PASSES, len(H_GROUPS) - 1)] // 16
            grouped = keep.tile([P, width, PACK], BF16, name="grouped%d" % u, align_bytes=64)
            for first, end, raw, r0 in raws[u]:
                cut = min(max(scalar_cols, first), end)
                if cut > first:
                    regroup(
                        nc.scalar.copy, grouped[:, first:cut, :], raw[:, :, r0 : r0 + cut - first]
                    )
                if end > cut:
                    regroup(
                        nc.vector.tensor_copy,
                        grouped[:, cut:end, :],
                        raw[:, :, r0 + cut - first : r0 + end - first],
                    )
            groupeds.append(grouped)

        def quantise_gradient(u):
            h0, width, c = units[u]
            nc.vector.quantize_mx(
                out=go_codes[:, c, h0 : h0 + width].bitcast(E5M2_X4),
                scales=go_scales[:, c, h0 : h0 + width],
                in_=groupeds[u][:].rearrange("p h j -> p (h j)"),
            )

        def multiply(u):
            h0, width, c = units[u]
            for t in range(h0 // H_TILE, (h0 + width) // H_TILE):
                if c == 0:
                    acc = psum.tile([P, OUT_F], F32, tag="bank%d" % t, name="acc%d" % t)
                    accs.append(acc)
                h_cols = slice(t * H_TILE, (t + 1) * H_TILE)
                nc.tensor.matmul_mx(
                    out=accs[t][:],
                    lhsT=go_codes[:, c, h_cols].bitcast(E5M2_X4),
                    lhsT_scale=go_scales[:, c, h_cols],
                    rhs=g_codes[:, c, :].bitcast(E4M3_X4),
                    rhs_scale=g_scales[:, c, :],
                    start=(c == 0),
                    stop=(c == PASSES - 1),
                )

        def empty_banks(u):
            h0, width, c = units[u]
            for t in range(h0 // H_TILE, (h0 + width) // H_TILE):
                result = keep.tile([P, DISTINCT_F], F32, name="result%d" % t)
                if t < H // H_TILE - 1:
                    nc.scalar.copy(out=result[:], in_=accs[t][:, 0:DISTINCT_F])
                else:
                    nc.vector.tensor_copy(out=result[:], in_=accs[t][:, 0:DISTINCT_F])
                rows = slice(t * H_TILE, (t + 1) * H_TILE)
                again = ATOM_F + ATOM_F - TWICE_FROM + BOND_F
                nc.sync.dma_start(out=out[rows, 0:ATOM_F], in_=result[:, 0:ATOM_F])
                nc.sync.dma_start(out=out[rows, ATOM_F:again], in_=result[:, TWICE_FROM:DISTINCT_F])
                nc.sync.dma_start(out=out[rows, again:OUT_F], in_=result[:, ATOM_F:DISTINCT_F])

        gate_atoms(0)
        regroup_unit(0)
        for step in range(len(units) + EMPTY_LAG):
            if step + 1 < PASSES:
                gate_atoms(step + 1)
            if step < PASSES:
                quantise_features(step)
            if step + 1 < len(units):
                regroup_unit(step + 1)
            if step < len(units):
                quantise_gradient(step)
                multiply(step)
            done = step - EMPTY_LAG
            if done >= 0 and units[done][2] == PASSES - 1:
                empty_banks(done)
